import numpy as np
import ml_dtypes


def mxq(x, axis, fmt="e4m3"):
    dtype, down = {"e4m3": (ml_dtypes.float8_e4m3fn, 7), "e5m2": (ml_dtypes.float8_e5m2, 14)}[fmt]
    v = np.moveaxis(np.asarray(x, np.float32).astype(ml_dtypes.bfloat16).astype(np.float64), axis, -1)
    blocks = v.reshape(v.shape[:-1] + (-1, 32))
    amax = np.abs(blocks).max(-1, keepdims=True)
    byte = np.maximum(np.where(amax > 0, np.frexp(amax)[1] - 1 + 127, 0) - down, 1)
    scale = np.exp2(byte - 127.0)
    codes = (blocks / scale).astype(np.float32).astype(dtype).astype(np.float64)
    return np.moveaxis((codes * scale).reshape(v.shape), -1, axis)


WIDE = False


def mx_kscale(k):
    if not WIDE:
        return np.ones(k)
    levels = np.array([10, -10, 5, -5, 0])
    a = np.random.permutation(np.resize(levels, k // 512 * 4)).reshape(k // 512, 4)
    idx = np.arange(k)
    return np.exp2(a[idx // 512, idx % 128 // 32])


BF16 = ml_dtypes.bfloat16


def bf(x):
    return np.asarray(x, np.float32).astype(BF16)


def f64(x):
    return np.asarray(x).astype(np.float64)


E2M1 = np.array([0.0, 0.5, 1.0, 1.5, 2.0, 3.0, 4.0, 6.0, -0.0, -0.5, -1.0, -1.5, -2.0, -3.0, -4.0, -6.0])


def pack_weight(w, fmt):
    k, n = w.shape
    w = f64(bf(w)).reshape(k // 32, 32, n)
    amax = np.abs(w).max(1)
    if fmt == "e4m3":
        byte = np.frexp(amax)[1] - 1 + 127 - 7
    else:
        mant, ex = np.frexp(amax / 6.0)
        byte = np.where(mant > 0.5, ex, ex - 1) + 127
    byte = np.clip(np.where(amax > 0, byte, 1), 1, 254)
    scaled = (w * np.exp2(127.0 - byte)[:, None, :]).reshape(k, n).astype(np.float32)
    by_word = np.ascontiguousarray(scaled.reshape(k // 512, 128, 4, n).transpose(0, 1, 3, 2))
    if fmt == "e4m3":
        words = by_word.astype(ml_dtypes.float8_e4m3fn).view(np.uint8)
    else:
        c = by_word.astype(ml_dtypes.float4_e2m1fn).view(np.uint8) & 0xF
        words = c[..., 0::2] | (c[..., 1::2] << 4)
    return np.ascontiguousarray(words), np.ascontiguousarray(byte.astype(np.uint8).reshape(k // 512, 16, n))


def unpack_weight(words, scales, fmt):
    g, p, n, _ = words.shape
    if fmt == "e4m3":
        vals = np.ascontiguousarray(words).view(ml_dtypes.float8_e4m3fn).astype(np.float64)
    else:
        nib = np.empty((g, p, n, 4), np.uint8)
        nib[..., 0::2] = words & 0xF
        nib[..., 1::2] = words >> 4
        vals = E2M1[nib]
    vals = vals * np.repeat(np.exp2(scales.astype(np.float64) - 127.0), 8, axis=1)[..., None]
    return vals.transpose(0, 1, 3, 2).reshape(g * 512, n)


B, M, D = 128, 4096, 2048
ALPHA = 0.5
TEMPERATURE = 0.07
FMT = "e4m3"


def l2norm(v):
    return v / np.sqrt((v * v).sum(-1, keepdims=True))


def setup_inputs():
    s = mx_kscale(D)
    c = np.sqrt(np.mean(s * s))
    x = bf(np.random.standard_normal((B, D)) * s)
    key_mem = np.random.standard_normal((M, D)) * (2.0 * TEMPERATURE) * c / s
    value_mem = np.random.standard_normal((M, D))
    key_mem_words, key_mem_scales = pack_weight(np.ascontiguousarray(key_mem.T), FMT)
    value_mem_words, value_mem_scales = pack_weight(value_mem, FMT)
    return {"x": x,
            "key_mem_words": key_mem_words, "key_mem_scales": key_mem_scales,
            "value_mem_words": value_mem_words, "value_mem_scales": value_mem_scales}


def reference(x, key_mem_words, key_mem_scales, value_mem_words, value_mem_scales):
    query = l2norm(f64(x))
    cosine_sim = mxq(query, 1, "e4m3") @ unpack_weight(key_mem_words, key_mem_scales, FMT)
    z = cosine_sim / TEMPERATURE
    e = np.exp(z - z.max(-1, keepdims=True))
    retrieved = (mxq(e, 1, "e4m3") @ unpack_weight(value_mem_words, value_mem_scales, FMT)) / e.sum(-1, keepdims=True)
    retrieved = l2norm(retrieved)
    interpolated = (1.0 - ALPHA) * query + ALPHA * retrieved
    return l2norm(interpolated)

@@ -1,0 +1,287 @@
+from contextlib import ExitStack
+
+import concourse.mybir as mybir
+from concourse.masks import make_identity
+
+F32 = mybir.dt.float32
+BF16 = mybir.dt.bfloat16
+U8 = mybir.dt.uint8
+U32 = mybir.dt.uint32
+I32 = mybir.dt.int32
+FP8X4 = mybir.dt.float8_e4m3fn_x4
+ALU = mybir.AluOpType
+ACT = mybir.ActivationFunctionType
+AX = mybir.AxisListType
+
+P = 128
+D = 2048
+M = 4096
+KG = D // 512
+VG = M // 512
+NT = 512
+NA = 3072
+TEMPERATURE = 0.07
+
+FLOPS = 2 * P * D * M * 2
+
+
+def tile_robustaugmentation_w_kernel(
+    tc, x, key_mem_words, key_mem_scales, value_mem_words, value_mem_scales, out
+):
+    nc = tc.nc
+    with ExitStack() as ctx:
+        keep = ctx.enter_context(tc.tile_pool(name="keep", bufs=1))
+        psum = ctx.enter_context(tc.psum_pool(name="psum", bufs=1))
+        ctx.enter_context(tc.manual_schedule())
+
+        def small(name, cols=1):
+            return keep.tile([P, cols], F32, name=name)
+
+        x_sb = keep.tile([P, D], BF16, name="x_sb")
+        ident = keep.tile([P, P], BF16, name="ident")
+        k_planes = keep.tile([P, M], U8, name="k_planes", align_bytes=64)
+        v_planes = keep.tile([P, 2 * D], U8, name="v_planes", align_bytes=64)
+        kw_a = [keep.tile([P, 4 * NA], U8, name="kw_a%d" % g, align_bytes=64) for g in range(KG)]
+        kw_b = keep.tile([P, KG - 1, 4 * (M - NA)], U8, name="kw_b", align_bytes=64)
+        kw_c = [keep.tile([P, 4 * NT], U8, name="kw_c%d" % j, align_bytes=64) for j in range(2)]
+        vw = [keep.tile([P, 4 * D], U8, name="vw%d" % g, align_bytes=64) for g in range(VG - 1)]
+        vw_l = [keep.tile([P, 4 * NT], U8, name="vw_l%d" % n, align_bytes=64) for n in range(4)]
+
+        one = small("one")
+        warm = small("warm")
+
+        nc.vector.memset(k_planes[:].bitcast(I32), 0)
+        nc.vector.memset(one[:], 1.0)
+        nc.vector.memset(v_planes[:].bitcast(I32), 0)
+        make_identity(nc, ident[:])
+        nc.scalar.activation(out=warm[:], in_=one[:], func=ACT.Sqrt)
+
+        def key_words(g, lo, hi):
+            return key_mem_words[g].rearrange("p n t -> p (n t)")[:, 4 * lo : 4 * hi].bitcast(I32)
+
+        def value_words(g, lo, hi):
+            return value_mem_words[g].rearrange("p n t -> p (n t)")[:, 4 * lo : 4 * hi].bitcast(I32)
+
+        def load_value_scales(h):
+            for q in (0, 2, 1, 3):
+                nc.sync.dma_start(
+                    out=v_planes[32 * q : 32 * q + 16, D * h : D * (h + 1)].bitcast(I32),
+                    in_=value_mem_scales[4 * h : 4 * h + 4, 4 * q : 4 * q + 4, :].bitcast(I32),
+                )
+
+        nc.sync.dma_start(out=x_sb[:], in_=x)
+        for q in (0, 2, 1, 3):
+            nc.sync.dma_start(
+                out=k_planes[32 * q : 32 * q + 16, :].bitcast(I32),
+                in_=key_mem_scales[:, 4 * q : 4 * q + 4, :].bitcast(I32),
+            )
+        for g in range(3):
+            nc.sync.dma_start(out=kw_a[g][:].bitcast(I32), in_=key_words(g, 0, NA))
+        load_value_scales(0)
+        nc.sync.dma_start(out=kw_a[3][:].bitcast(I32), in_=key_words(3, 0, NA))
+        load_value_scales(1)
+        nc.sync.dma_start(
+            out=kw_b[:].bitcast(I32),
+            in_=key_mem_words[0 : KG - 1].rearrange("g p n t -> p g (n t)")[:, :, 4 * NA :].bitcast(I32),
+        )
+        for j in range(2):
+            nc.sync.dma_start(
+                out=kw_c[j][:].bitcast(I32), in_=key_words(3, NA + NT * j, NA + NT * (j + 1))
+            )
+        for g in range(VG - 1):
+            nc.sync.dma_start(out=vw[g][:].bitcast(I32), in_=value_words(g, 0, D))
+        for n in range(4):
+            nc.sync.dma_start(
+                out=vw_l[n][:].bitcast(I32), in_=value_words(VG - 1, NT * n, NT * (n + 1))
+            )
+
+        ss_s = small("ss_s")
+        ss_v = small("ss_v")
+        norm = small("norm")
+        rn = small("rn")
+        junk_s = keep.tile([P, D // 2], BF16, name="junk_s")
+        junk_v = keep.tile([P, D // 2], F32, name="junk_v")
+        half = D // 2
+        nc.scalar.activation(out=junk_s[:], in_=x_sb[:, 0:half], func=ACT.Square, accum_out=ss_s[:])
+        nc.vector.scalar_tensor_tensor(
+            out=junk_v[:], in0=x_sb[:, half:D], scalar=1.0, in1=x_sb[:, half:D],
+            op0=ALU.mult, op1=ALU.mult, accum_out=ss_v[:],
+        )
+        nc.scalar.activation(out=norm[:], in_=ss_s[:], func=ACT.Sqrt, bias=ss_v[:])
+        nc.vector.reciprocal(out=rn[:], in_=norm[:])
+
+        q_bf = [keep.tile([P, 512], BF16, name="q_bf%d" % g) for g in range(KG)]
+        q_t = [psum.tile([P, 4, P], BF16, name="q_t%d" % g, tag="bank%d" % g) for g in range(KG)]
+        q_grp = [keep.tile([P, 1024], BF16, name="q_grp%d" % h, align_bytes=64) for h in range(2)]
+        q_codes = [keep.tile([P, 256], U32, name="q_codes%d" % h, align_bytes=64) for h in range(2)]
+        q_plane = [keep.tile([P, 256], U8, name="q_plane%d" % h, align_bytes=64) for h in range(2)]
+
+        def sorted_view(ap):
+            return ap.rearrange("b (t p) -> b t p", t=4)
+
+        def natural_view(ap):
+            return ap.rearrange("b (p t) -> b t p", t=4)
+
+        def scale_query(g):
+            src = natural_view(x_sb[:, 512 * g : 512 * (g + 1)])
+            dst = sorted_view(q_bf[g][:])
+            if g < 2:
+                nc.vector.tensor_scalar(out=dst, in0=src, scalar1=rn[:], scalar2=None, op0=ALU.mult)
+            else:
+                nc.scalar.activation(out=dst, in_=src, func=ACT.Copy, scale=rn[:])
+
+        def transpose_four(dst, src):
+            for t in range(4):
+                nc.tensor.transpose(out=dst[:, t, :], in_=src[:, P * t : P * (t + 1)], identity=ident[:])
+
+        def group_query(g):
+            dst = q_grp[g // 2][:, 512 * (g % 2) : 512 * (g % 2 + 1)].rearrange("p (b t) -> p b t", t=4)
+            src = q_t[g][:].rearrange("p t b -> p b t")
+            if g < 2:
+                nc.vector.tensor_copy(out=dst, in_=src)
+            else:
+                nc.scalar.copy(out=dst, in_=src)
+
+        for g in (0, 2, 1, 3):
+            scale_query(g)
+            transpose_four(q_t[g], q_bf[g])
+        for g in (0, 2, 1, 3):
+            group_query(g)
+        for h in range(2):
+            nc.vector.quantize_mx(out=q_codes[h][:].bitcast(FP8X4), scales=q_plane[h][:], in_=q_grp[h][:])
+
+        q32 = keep.tile([P, D], F32, name="q32")
+        nc.scalar.activation(out=q32[:], in_=x_sb[:], func=ACT.Copy, scale=rn[:])
+        nc.scalar.activation(out=warm[:], in_=one[:], func=ACT.Exp)
+
+        z = [psum.tile([P, NT], F32, name="z%d" % j, tag="bank%d" % j) for j in range(8)]
+        zs = [keep.tile([P, NT], F32, name="zs%d" % j) for j in range(8)]
+        nb = small("nb", 8)
+
+        def key_pass(j, g, rhs):
+            nc.tensor.matmul_mx(
+                out=z[j][:],
+                lhsT=q_codes[g // 2][:, P * (g % 2) : P * (g % 2 + 1)].bitcast(FP8X4),
+                lhsT_scale=q_plane[g // 2][:, P * (g % 2) : P * (g % 2 + 1)],
+                rhs=rhs.bitcast(FP8X4),
+                rhs_scale=k_planes[4 * g : P, NT * j : NT * (j + 1)],
+                start=(g == 0),
+                stop=(g == KG - 1),
+            )
+
+        def leave_bank(j):
+            nc.vector.tensor_scalar(
+                out=sorted_view(zs[j][:]),
+                in0=natural_view(z[j][:]),
+                scalar1=-1.0 / TEMPERATURE,
+                scalar2=(None if j == 0 else nb[:, j - 1 : j]),
+                op0=ALU.mult,
+                op1=ALU.min,
+                accum_out=nb[:, j : j + 1],
+            )
+
+        na_banks = NA // NT
+        for g in range(KG):
+            for j in range(na_banks):
+                key_pass(j, g, kw_a[g][:, 4 * NT * j : 4 * NT * (j + 1)])
+        for j in range(na_banks):
+            leave_bank(j)
+        for g in range(KG - 1):
+            for j in range(na_banks, 8):
+                key_pass(j, g, kw_b[:, g, 4 * NT * (j - na_banks) : 4 * NT * (j - na_banks + 1)])
+        for j in range(na_banks, 8):
+            key_pass(j, KG - 1, kw_c[j - na_banks][:])
+            leave_bank(j)
+
+        e_sb = [keep.tile([P, 512], BF16, name="e_sb%d" % g) for g in range(VG)]
+        e_grp = [keep.tile([P, 512], BF16, name="e_grp%d" % g, align_bytes=64) for g in range(VG)]
+        e_codes = [keep.tile([P, P], U32, name="e_codes%d" % g, align_bytes=64) for g in range(VG)]
+        e_plane = [keep.tile([P, P], U8, name="e_plane%d" % g, align_bytes=64) for g in range(VG)]
+        e_t = {}
+        r = [psum.tile([P, NT], F32, name="r%d" % n, tag="bank%d" % n) for n in range(4)]
+
+        def exp_and_transpose(g):
+            nc.scalar.activation(out=e_sb[g][:], in_=zs[g][:], func=ACT.Exp, scale=-1.0, bias=nb[:, 7:8])
+            e_t[g] = psum.tile([P, 4, P], BF16, name="e_t%d" % g, tag="bank%d" % (4 + g % 4))
+            transpose_four(e_t[g], e_sb[g])
+
+        def group_e(g):
+            nc.vector.tensor_copy(
+                out=e_grp[g][:].rearrange("p (b t) -> p b t", t=4),
+                in_=e_t[g][:].rearrange("p t b -> p b t"),
+            )
+
+        def quantise_e(g):
+            nc.vector.quantize_mx(out=e_codes[g][:].bitcast(FP8X4), scales=e_plane[g][:], in_=e_grp[g][:])
+
+        def value_pass(n, g, rhs):
+            nc.tensor.matmul_mx(
+                out=r[n][:],
+                lhsT=e_codes[g][:].bitcast(FP8X4),
+                lhsT_scale=e_plane[g][:],
+                rhs=rhs.bitcast(FP8X4),
+                rhs_scale=v_planes[4 * (g % 4) : P, D * (g // 4) + NT * n : D * (g // 4) + NT * (n + 1)],
+                start=(g == 0),
+                stop=(g == VG - 1),
+            )
+
+        def four_chunks(first):
+            for g in range(first, first + 4):
+                exp_and_transpose(g)
+            group_e(first)
+            group_e(first + 1)
+            quantise_e(first)
+            group_e(first + 2)
+            quantise_e(first + 1)
+            group_e(first + 3)
+            quantise_e(first + 2)
+            quantise_e(first + 3)
+
+        four_chunks(0)
+        for g in (0, 1):
+            for n in range(4):
+                value_pass(n, g, vw[g][:, 4 * NT * n : 4 * NT * (n + 1)])
+        four_chunks(4)
+        nc.scalar.activation(out=warm[:], in_=one[:], func=ACT.Sqrt)
+        for g in range(2, VG - 1):
+            for n in range(4):
+                value_pass(n, g, vw[g][:, 4 * NT * n : 4 * NT * (n + 1)])
+
+        rr = small("rr", 4)
+        qr = small("qr", 4)
+        rr_head = small("rr_head")
+        rho = small("rho")
+        qr_sum = small("qr_sum")
+        v2 = small("v2")
+        root = small("root")
+        beta = small("beta")
+        w = [keep.tile([P, NT], F32, name="w%d" % n) for n in range(4)]
+
+        for n in range(4):
+            value_pass(n, VG - 1, vw_l[n][:])
+            nc.scalar.activation(out=junk_s[:, 0:NT], in_=r[n][:], func=ACT.Square, accum_out=rr[:, n : n + 1])
+            if n == 2:
+                nc.vector.reduce_sum(out=rr_head[:], in_=rr[:, 0:3], axis=AX.X)
+            if n == 3:
+                nc.scalar.activation(out=rho[:], in_=rr[:, 3:4], func=ACT.Sqrt, bias=rr_head[:])
+            nc.vector.scalar_tensor_tensor(
+                out=junk_v[:, 0:NT], in0=r[n][:], scalar=1.0, in1=q32[:, NT * n : NT * (n + 1)],
+                op0=ALU.mult, op1=ALU.mult, accum_out=qr[:, n : n + 1],
+            )
+        nc.vector.reduce_sum(out=qr_sum[:], in_=qr[:], axis=AX.X)
+        nc.vector.tensor_scalar(
+            out=v2[:], in0=qr_sum[:], scalar1=rho[:], scalar2=rho[:], op0=ALU.add, op1=ALU.mult
+        )
+        nc.scalar.activation(out=root[:], in_=v2[:], func=ACT.Sqrt, scale=2.0)
+        for n in range(4):
+            nc.vector.scalar_tensor_tensor(
+                out=w[n][:], in0=q32[:, NT * n : NT * (n + 1)], scalar=rho[:], in1=r[n][:],
+                op0=ALU.mult, op1=ALU.add,
+            )
+            if n == 0:
+                nc.vector.reciprocal(out=beta[:], in_=root[:])
+            if n < 3:
+                nc.scalar.activation(out=w[n][:], in_=w[n][:], func=ACT.Copy, scale=beta[:])
+            else:
+                nc.vector.tensor_scalar(out=w[n][:], in0=w[n][:], scalar1=beta[:], scalar2=None, op0=ALU.mult)
+            nc.sync.dma_start(out=out[:, NT * n : NT * (n + 1)], in_=w[n][:])

@@ -62,11 +62,14 @@ def tile_robustaugmentation_w_kernel(
         def value_words(g, lo, hi):
             return value_mem_words[g].rearrange("p n t -> p (n t)")[:, 4 * lo : 4 * hi].bitcast(I32)
 
-        def load_value_scales(h):
+        scale_rows = value_mem_scales.rearrange("(h j) q n -> j q h n", j=4)
+        for r4 in range(4):
             for q in (0, 2, 1, 3):
-                nc.sync.dma_start(
-                    out=v_planes[32 * q : 32 * q + 16, D * h : D * (h + 1)].bitcast(I32),
-                    in_=value_mem_scales[4 * h : 4 * h + 4, 4 * q : 4 * q + 4, :].bitcast(I32),
+                nc.gpsimd.dma_start(
+                    out=v_planes[32 * q + r4 : 32 * q + 16 : 4, :]
+                    .rearrange("p (h n) -> p h n", h=2)
+                    .bitcast(F32),
+                    in_=scale_rows[:, 4 * q + r4].bitcast(F32),
                 )
 
         nc.sync.dma_start(out=x_sb[:], in_=x)
@@ -77,9 +80,7 @@ def tile_robustaugmentation_w_kernel(
             )
         for g in range(3):
             nc.sync.dma_start(out=kw_a[g][:].bitcast(I32), in_=key_words(g, 0, NA))
-        load_value_scales(0)
         nc.sync.dma_start(out=kw_a[3][:].bitcast(I32), in_=key_words(3, 0, NA))
-        load_value_scales(1)
         nc.sync.dma_start(
             out=kw_b[:].bitcast(I32),
             in_=key_mem_words[0 : KG - 1].rearrange("g p n t -> p g (n t)")[:, :, 4 * NA :].bitcast(I32),

@@ -21,6 +21,7 @@ VG = M // 512
 NT = 512
 NA = 3072
 TEMPERATURE = 0.07
+TILES = ((0, 512), (512, 512), (1024, 512), (1536, 256), (1792, 256))
 
 FLOPS = 2 * P * D * M * 2
 
@@ -44,8 +45,9 @@ def tile_robustaugmentation_w_kernel(
         kw_a = [keep.tile([P, 4 * NA], U8, name="kw_a%d" % g, align_bytes=64) for g in range(KG)]
         kw_b = keep.tile([P, KG - 1, 4 * (M - NA)], U8, name="kw_b", align_bytes=64)
         kw_c = [keep.tile([P, 4 * NT], U8, name="kw_c%d" % j, align_bytes=64) for j in range(2)]
-        vw = [keep.tile([P, 4 * D], U8, name="vw%d" % g, align_bytes=64) for g in range(VG - 1)]
-        vw_l = [keep.tile([P, 4 * NT], U8, name="vw_l%d" % n, align_bytes=64) for n in range(4)]
+        vw = [keep.tile([P, 4 * D], U8, name="vw%d" % g, align_bytes=64) for g in range(VG - 2)]
+        v_end = [keep.tile([P, 2, 4 * NT], U8, name="v_end%d" % n, align_bytes=64) for n in range(3)]
+        v_last = [keep.tile([P, 4 * NT], U8, name="v_last%d" % i, align_bytes=64) for i in range(2)]
 
         one = small("one")
         warm = small("warm")
@@ -62,14 +64,11 @@ def tile_robustaugmentation_w_kernel(
         def value_words(g, lo, hi):
             return value_mem_words[g].rearrange("p n t -> p (n t)")[:, 4 * lo : 4 * hi].bitcast(I32)
 
-        scale_rows = value_mem_scales.rearrange("(h j) q n -> j q h n", j=4)
-        for r4 in range(4):
+        def load_value_scales(h):
             for q in (0, 2, 1, 3):
-                nc.gpsimd.dma_start(
-                    out=v_planes[32 * q + r4 : 32 * q + 16 : 4, :]
-                    .rearrange("p (h n) -> p h n", h=2)
-                    .bitcast(F32),
-                    in_=scale_rows[:, 4 * q + r4].bitcast(F32),
+                nc.sync.dma_start(
+                    out=v_planes[32 * q : 32 * q + 16, D * h : D * (h + 1)].bitcast(I32),
+                    in_=value_mem_scales[4 * h : 4 * h + 4, 4 * q : 4 * q + 4, :].bitcast(I32),
                 )
 
         nc.sync.dma_start(out=x_sb[:], in_=x)
@@ -78,9 +77,8 @@ def tile_robustaugmentation_w_kernel(
                 out=k_planes[32 * q : 32 * q + 16, :].bitcast(I32),
                 in_=key_mem_scales[:, 4 * q : 4 * q + 4, :].bitcast(I32),
             )
-        for g in range(3):
+        for g in range(KG):
             nc.sync.dma_start(out=kw_a[g][:].bitcast(I32), in_=key_words(g, 0, NA))
-        nc.sync.dma_start(out=kw_a[3][:].bitcast(I32), in_=key_words(3, 0, NA))
         nc.sync.dma_start(
             out=kw_b[:].bitcast(I32),
             in_=key_mem_words[0 : KG - 1].rearrange("g p n t -> p g (n t)")[:, :, 4 * NA :].bitcast(I32),
@@ -89,12 +87,19 @@ def tile_robustaugmentation_w_kernel(
             nc.sync.dma_start(
                 out=kw_c[j][:].bitcast(I32), in_=key_words(3, NA + NT * j, NA + NT * (j + 1))
             )
-        for g in range(VG - 1):
+        load_value_scales(0)
+        for g in range(4):
             nc.sync.dma_start(out=vw[g][:].bitcast(I32), in_=value_words(g, 0, D))
-        for n in range(4):
+        load_value_scales(1)
+        for g in range(4, VG - 2):
+            nc.sync.dma_start(out=vw[g][:].bitcast(I32), in_=value_words(g, 0, D))
+        last_two = value_mem_words[VG - 2 : VG].rearrange("g p n t -> p g (n t)")
+        for n in range(3):
             nc.sync.dma_start(
-                out=vw_l[n][:].bitcast(I32), in_=value_words(VG - 1, NT * n, NT * (n + 1))
+                out=v_end[n][:].bitcast(I32), in_=last_two[:, :, 4 * NT * n : 4 * NT * (n + 1)].bitcast(I32)
             )
+        for i in range(2):
+            nc.sync.dma_start(out=v_last[i][:].bitcast(I32), in_=value_words(VG - 2 + i, 3 * NT, D))
 
         ss_s = small("ss_s")
         ss_v = small("ss_v")
@@ -195,62 +200,66 @@ def tile_robustaugmentation_w_kernel(
             leave_bank(j)
 
         e_sb = [keep.tile([P, 512], BF16, name="e_sb%d" % g) for g in range(VG)]
-        e_grp = [keep.tile([P, 512], BF16, name="e_grp%d" % g, align_bytes=64) for g in range(VG)]
-        e_codes = [keep.tile([P, P], U32, name="e_codes%d" % g, align_bytes=64) for g in range(VG)]
-        e_plane = [keep.tile([P, P], U8, name="e_plane%d" % g, align_bytes=64) for g in range(VG)]
+        e_grp = [keep.tile([P, 1024], BF16, name="e_grp%d" % u, align_bytes=64) for u in range(4)]
+        e_codes = [keep.tile([P, 2 * P], U32, name="e_codes%d" % u, align_bytes=64) for u in range(4)]
+        e_plane = [keep.tile([P, 2 * P], U8, name="e_plane%d" % u, align_bytes=64) for u in range(4)]
         e_t = {}
-        r = [psum.tile([P, NT], F32, name="r%d" % n, tag="bank%d" % n) for n in range(4)]
+        r = [psum.tile([P, TILES[n][1]], F32, name="r%d" % n, tag="bank%d" % n) for n in range(5)]
 
         def exp_and_transpose(g):
             nc.scalar.activation(out=e_sb[g][:], in_=zs[g][:], func=ACT.Exp, scale=-1.0, bias=nb[:, 7:8])
-            e_t[g] = psum.tile([P, 4, P], BF16, name="e_t%d" % g, tag="bank%d" % (4 + g % 4))
-            transpose_four(e_t[g], e_sb[g])
+            u = g // 2
+            if g % 2 == 0:
+                e_t[u] = psum.tile([P, 2, 4, P], BF16, name="e_t%d" % u, tag="bank%d" % (5 + u % 3))
+            transpose_four(e_t[u][:, g % 2], e_sb[g])
 
-        def group_e(g):
+        def group_e(u):
             nc.vector.tensor_copy(
-                out=e_grp[g][:].rearrange("p (b t) -> p b t", t=4),
-                in_=e_t[g][:].rearrange("p t b -> p b t"),
+                out=e_grp[u][:].rearrange("p (g b t) -> p g b t", g=2, t=4),
+                in_=e_t[u][:].rearrange("p g t b -> p g b t"),
             )
 
-        def quantise_e(g):
-            nc.vector.quantize_mx(out=e_codes[g][:].bitcast(FP8X4), scales=e_plane[g][:], in_=e_grp[g][:])
+        def quantise_e(u):
+            nc.vector.quantize_mx(out=e_codes[u][:].bitcast(FP8X4), scales=e_plane[u][:], in_=e_grp[u][:])
 
         def value_pass(n, g, rhs):
+            c0, wd = TILES[n]
+            col = D * (g // 4) + c0
             nc.tensor.matmul_mx(
                 out=r[n][:],
-                lhsT=e_codes[g][:].bitcast(FP8X4),
-                lhsT_scale=e_plane[g][:],
+                lhsT=e_codes[g // 2][:, P * (g % 2) : P * (g % 2 + 1)].bitcast(FP8X4),
+                lhsT_scale=e_plane[g // 2][:, P * (g % 2) : P * (g % 2 + 1)],
                 rhs=rhs.bitcast(FP8X4),
-                rhs_scale=v_planes[4 * (g % 4) : P, D * (g // 4) + NT * n : D * (g // 4) + NT * (n + 1)],
+                rhs_scale=v_planes[4 * (g % 4) : P, col : col + wd],
                 start=(g == 0),
                 stop=(g == VG - 1),
             )
 
+        def whole_group(g):
+            for n in range(5):
+                c0, wd = TILES[n]
+                value_pass(n, g, vw[g][:, 4 * c0 : 4 * (c0 + wd)])
+
         def four_chunks(first):
             for g in range(first, first + 4):
                 exp_and_transpose(g)
-            group_e(first)
-            group_e(first + 1)
-            quantise_e(first)
-            group_e(first + 2)
-            quantise_e(first + 1)
-            group_e(first + 3)
-            quantise_e(first + 2)
-            quantise_e(first + 3)
+            group_e(first // 2)
+            group_e(first // 2 + 1)
+            quantise_e(first // 2)
+            quantise_e(first // 2 + 1)
 
         four_chunks(0)
-        for g in (0, 1):
-            for n in range(4):
-                value_pass(n, g, vw[g][:, 4 * NT * n : 4 * NT * (n + 1)])
+        whole_group(0)
+        whole_group(1)
         four_chunks(4)
         nc.scalar.activation(out=warm[:], in_=one[:], func=ACT.Sqrt)
-        for g in range(2, VG - 1):
-            for n in range(4):
-                value_pass(n, g, vw[g][:, 4 * NT * n : 4 * NT * (n + 1)])
+        for g in range(2, VG - 2):
+            whole_group(g)
 
-        rr = small("rr", 4)
-        qr = small("qr", 4)
+        rr = small("rr", 5)
+        qr = small("qr", 5)
         rr_head = small("rr_head")
+        rr_most = small("rr_most")
         rho = small("rho")
         qr_sum = small("qr_sum")
         v2 = small("v2")
@@ -258,31 +267,55 @@ def tile_robustaugmentation_w_kernel(
         beta = small("beta")
         w = [keep.tile([P, NT], F32, name="w%d" % n) for n in range(4)]
 
-        for n in range(4):
-            value_pass(n, VG - 1, vw_l[n][:])
-            nc.scalar.activation(out=junk_s[:, 0:NT], in_=r[n][:], func=ACT.Square, accum_out=rr[:, n : n + 1])
-            if n == 2:
-                nc.vector.reduce_sum(out=rr_head[:], in_=rr[:, 0:3], axis=AX.X)
-            if n == 3:
-                nc.scalar.activation(out=rho[:], in_=rr[:, 3:4], func=ACT.Sqrt, bias=rr_head[:])
+        def q_cols(n):
+            c0, wd = TILES[n]
+            return q32[:, c0 : c0 + wd]
+
+        def w_cols(n):
+            c0, wd = TILES[n]
+            return w[c0 // NT][:, c0 % NT : c0 % NT + wd]
+
+        def sum_squares(n):
+            wd = TILES[n][1]
+            nc.scalar.activation(out=junk_s[:, 0:wd], in_=r[n][:], func=ACT.Square, accum_out=rr[:, n : n + 1])
+
+        def dot_query(n):
+            wd = TILES[n][1]
             nc.vector.scalar_tensor_tensor(
-                out=junk_v[:, 0:NT], in0=r[n][:], scalar=1.0, in1=q32[:, NT * n : NT * (n + 1)],
+                out=junk_v[:, 0:wd], in0=r[n][:], scalar=1.0, in1=q_cols(n),
                 op0=ALU.mult, op1=ALU.mult, accum_out=qr[:, n : n + 1],
             )
+
+        for n in range(3):
+            for i in range(2):
+                value_pass(n, VG - 2 + i, v_end[n][:, i, :])
+            sum_squares(n)
+            if n == 2:
+                nc.vector.reduce_sum(out=rr_head[:], in_=rr[:, 0:3], axis=AX.X)
+            dot_query(n)
+        for i in range(2):
+            for n in (3, 4):
+                c0, wd = TILES[n]
+                value_pass(n, VG - 2 + i, v_last[i][:, 4 * (c0 - 3 * NT) : 4 * (c0 - 3 * NT + wd)])
+        sum_squares(3)
+        nc.vector.tensor_scalar(out=rr_most[:], in0=rr[:, 3:4], scalar1=rr_head[:], scalar2=None, op0=ALU.add)
+        sum_squares(4)
+        nc.scalar.activation(out=rho[:], in_=rr[:, 4:5], func=ACT.Sqrt, bias=rr_most[:])
+        dot_query(3)
+        dot_query(4)
         nc.vector.reduce_sum(out=qr_sum[:], in_=qr[:], axis=AX.X)
         nc.vector.tensor_scalar(
             out=v2[:], in0=qr_sum[:], scalar1=rho[:], scalar2=rho[:], op0=ALU.add, op1=ALU.mult
         )
         nc.scalar.activation(out=root[:], in_=v2[:], func=ACT.Sqrt, scale=2.0)
-        for n in range(4):
+        for n in range(5):
             nc.vector.scalar_tensor_tensor(
-                out=w[n][:], in0=q32[:, NT * n : NT * (n + 1)], scalar=rho[:], in1=r[n][:],
-                op0=ALU.mult, op1=ALU.add,
+                out=w_cols(n), in0=q_cols(n), scalar=rho[:], in1=r[n][:], op0=ALU.mult, op1=ALU.add
             )
             if n == 0:
                 nc.vector.reciprocal(out=beta[:], in_=root[:])
             if n < 3:
                 nc.scalar.activation(out=w[n][:], in_=w[n][:], func=ACT.Copy, scale=beta[:])
-            else:
-                nc.vector.tensor_scalar(out=w[n][:], in0=w[n][:], scalar1=beta[:], scalar2=None, op0=ALU.mult)
-            nc.sync.dma_start(out=out[:, NT * n : NT * (n + 1)], in_=w[n][:])
+                nc.sync.dma_start(out=out[:, NT * n : NT * (n + 1)], in_=w[n][:])
+        nc.vector.tensor_scalar(out=w[3][:], in0=w[3][:], scalar1=beta[:], scalar2=None, op0=ALU.mult)
+        nc.sync.dma_start(out=out[:, 3 * NT : D], in_=w[3][:])

@@ -47,7 +47,8 @@ def tile_robustaugmentation_w_kernel(
         kw_c = [keep.tile([P, 4 * NT], U8, name="kw_c%d" % j, align_bytes=64) for j in range(2)]
         vw = [keep.tile([P, 4 * D], U8, name="vw%d" % g, align_bytes=64) for g in range(VG - 2)]
         v_end = [keep.tile([P, 2, 4 * NT], U8, name="v_end%d" % n, align_bytes=64) for n in range(3)]
-        v_last = [keep.tile([P, 4 * NT], U8, name="v_last%d" % i, align_bytes=64) for i in range(2)]
+        v_six = keep.tile([P, 4 * NT], U8, name="v_six", align_bytes=64)
+        v_seven = [keep.tile([P, 2 * NT], U8, name="v_seven%d" % i, align_bytes=64) for i in range(2)]
 
         one = small("one")
         warm = small("warm")
@@ -72,12 +73,13 @@ def tile_robustaugmentation_w_kernel(
                 )
 
         nc.sync.dma_start(out=x_sb[:], in_=x)
+        nc.sync.dma_start(out=kw_a[0][:].bitcast(I32), in_=key_words(0, 0, NA))
         for q in (0, 2, 1, 3):
             nc.sync.dma_start(
                 out=k_planes[32 * q : 32 * q + 16, :].bitcast(I32),
                 in_=key_mem_scales[:, 4 * q : 4 * q + 4, :].bitcast(I32),
             )
-        for g in range(KG):
+        for g in range(1, KG):
             nc.sync.dma_start(out=kw_a[g][:].bitcast(I32), in_=key_words(g, 0, NA))
         nc.sync.dma_start(
             out=kw_b[:].bitcast(I32),
@@ -98,8 +100,12 @@ def tile_robustaugmentation_w_kernel(
             nc.sync.dma_start(
                 out=v_end[n][:].bitcast(I32), in_=last_two[:, :, 4 * NT * n : 4 * NT * (n + 1)].bitcast(I32)
             )
-        for i in range(2):
-            nc.sync.dma_start(out=v_last[i][:].bitcast(I32), in_=value_words(VG - 2 + i, 3 * NT, D))
+        nc.sync.dma_start(out=v_six[:].bitcast(I32), in_=value_words(VG - 2, 3 * NT, D))
+        for n in (3, 4):
+            nc.sync.dma_start(
+                out=v_seven[n - 3][:].bitcast(I32),
+                in_=value_words(VG - 1, TILES[n][0], TILES[n][0] + TILES[n][1]),
+            )
 
         ss_s = small("ss_s")
         ss_v = small("ss_v")
@@ -293,10 +299,11 @@ def tile_robustaugmentation_w_kernel(
             if n == 2:
                 nc.vector.reduce_sum(out=rr_head[:], in_=rr[:, 0:3], axis=AX.X)
             dot_query(n)
-        for i in range(2):
-            for n in (3, 4):
-                c0, wd = TILES[n]
-                value_pass(n, VG - 2 + i, v_last[i][:, 4 * (c0 - 3 * NT) : 4 * (c0 - 3 * NT + wd)])
+        for n in (3, 4):
+            c0, wd = TILES[n]
+            value_pass(n, VG - 2, v_six[:, 4 * (c0 - 3 * NT) : 4 * (c0 - 3 * NT + wd)])
+        for n in (3, 4):
+            value_pass(n, VG - 1, v_seven[n - 3][:])
         sum_squares(3)
         nc.vector.tensor_scalar(out=rr_most[:], in0=rr[:, 3:4], scalar1=rr_head[:], scalar2=None, op0=ALU.add)
         sum_squares(4)
@@ -314,8 +321,14 @@ def tile_robustaugmentation_w_kernel(
             )
             if n == 0:
                 nc.vector.reciprocal(out=beta[:], in_=root[:])
-            if n < 3:
-                nc.scalar.activation(out=w[n][:], in_=w[n][:], func=ACT.Copy, scale=beta[:])
-                nc.sync.dma_start(out=out[:, NT * n : NT * (n + 1)], in_=w[n][:])
-        nc.vector.tensor_scalar(out=w[3][:], in0=w[3][:], scalar1=beta[:], scalar2=None, op0=ALU.mult)
-        nc.sync.dma_start(out=out[:, 3 * NT : D], in_=w[3][:])
+            if n == 1:
+                nc.gpsimd.tensor_scalar(
+                    out=w_cols(n), in0=w_cols(n), scalar1=beta[:], scalar2=0.0, op0=ALU.mult, op1=ALU.add
+                )
+            elif n < 3:
+                nc.scalar.activation(out=w_cols(n), in_=w_cols(n), func=ACT.Copy, scale=beta[:])
+            else:
+                nc.vector.tensor_scalar(
+                    out=w_cols(n), in0=w_cols(n), scalar1=beta[:], scalar2=None, op0=ALU.mult
+                )
+            nc.sync.dma_start(out=out[:, TILES[n][0] : TILES[n][0] + TILES[n][1]], in_=w_cols(n))

@@ -47,8 +47,7 @@ def tile_robustaugmentation_w_kernel(
         kw_c = [keep.tile([P, 4 * NT], U8, name="kw_c%d" % j, align_bytes=64) for j in range(2)]
         vw = [keep.tile([P, 4 * D], U8, name="vw%d" % g, align_bytes=64) for g in range(VG - 2)]
         v_end = [keep.tile([P, 2, 4 * NT], U8, name="v_end%d" % n, align_bytes=64) for n in range(3)]
-        v_six = keep.tile([P, 4 * NT], U8, name="v_six", align_bytes=64)
-        v_seven = [keep.tile([P, 2 * NT], U8, name="v_seven%d" % i, align_bytes=64) for i in range(2)]
+        v_last = [keep.tile([P, 4 * NT], U8, name="v_last%d" % i, align_bytes=64) for i in range(2)]
 
         one = small("one")
         warm = small("warm")
@@ -73,13 +72,12 @@ def tile_robustaugmentation_w_kernel(
                 )
 
         nc.sync.dma_start(out=x_sb[:], in_=x)
-        nc.sync.dma_start(out=kw_a[0][:].bitcast(I32), in_=key_words(0, 0, NA))
         for q in (0, 2, 1, 3):
             nc.sync.dma_start(
                 out=k_planes[32 * q : 32 * q + 16, :].bitcast(I32),
                 in_=key_mem_scales[:, 4 * q : 4 * q + 4, :].bitcast(I32),
             )
-        for g in range(1, KG):
+        for g in range(KG):
             nc.sync.dma_start(out=kw_a[g][:].bitcast(I32), in_=key_words(g, 0, NA))
         nc.sync.dma_start(
             out=kw_b[:].bitcast(I32),
@@ -100,12 +98,8 @@ def tile_robustaugmentation_w_kernel(
             nc.sync.dma_start(
                 out=v_end[n][:].bitcast(I32), in_=last_two[:, :, 4 * NT * n : 4 * NT * (n + 1)].bitcast(I32)
             )
-        nc.sync.dma_start(out=v_six[:].bitcast(I32), in_=value_words(VG - 2, 3 * NT, D))
-        for n in (3, 4):
-            nc.sync.dma_start(
-                out=v_seven[n - 3][:].bitcast(I32),
-                in_=value_words(VG - 1, TILES[n][0], TILES[n][0] + TILES[n][1]),
-            )
+        for i in range(2):
+            nc.sync.dma_start(out=v_last[i][:].bitcast(I32), in_=value_words(VG - 2 + i, 3 * NT, D))
 
         ss_s = small("ss_s")
         ss_v = small("ss_v")
@@ -250,8 +244,8 @@ def tile_robustaugmentation_w_kernel(
             for g in range(first, first + 4):
                 exp_and_transpose(g)
             group_e(first // 2)
-            group_e(first // 2 + 1)
             quantise_e(first // 2)
+            group_e(first // 2 + 1)
             quantise_e(first // 2 + 1)
 
         four_chunks(0)
@@ -299,11 +293,10 @@ def tile_robustaugmentation_w_kernel(
             if n == 2:
                 nc.vector.reduce_sum(out=rr_head[:], in_=rr[:, 0:3], axis=AX.X)
             dot_query(n)
-        for n in (3, 4):
-            c0, wd = TILES[n]
-            value_pass(n, VG - 2, v_six[:, 4 * (c0 - 3 * NT) : 4 * (c0 - 3 * NT + wd)])
-        for n in (3, 4):
-            value_pass(n, VG - 1, v_seven[n - 3][:])
+        for i in range(2):
+            for n in (3, 4):
+                c0, wd = TILES[n]
+                value_pass(n, VG - 2 + i, v_last[i][:, 4 * (c0 - 3 * NT) : 4 * (c0 - 3 * NT + wd)])
         sum_squares(3)
         nc.vector.tensor_scalar(out=rr_most[:], in0=rr[:, 3:4], scalar1=rr_head[:], scalar2=None, op0=ALU.add)
         sum_squares(4)
@@ -321,14 +314,8 @@ def tile_robustaugmentation_w_kernel(
             )
             if n == 0:
                 nc.vector.reciprocal(out=beta[:], in_=root[:])
-            if n == 1:
-                nc.gpsimd.tensor_scalar(
-                    out=w_cols(n), in0=w_cols(n), scalar1=beta[:], scalar2=0.0, op0=ALU.mult, op1=ALU.add
-                )
-            elif n < 3:
-                nc.scalar.activation(out=w_cols(n), in_=w_cols(n), func=ACT.Copy, scale=beta[:])
-            else:
-                nc.vector.tensor_scalar(
-                    out=w_cols(n), in0=w_cols(n), scalar1=beta[:], scalar2=None, op0=ALU.mult
-                )
-            nc.sync.dma_start(out=out[:, TILES[n][0] : TILES[n][0] + TILES[n][1]], in_=w_cols(n))
+            if n < 3:
+                nc.scalar.activation(out=w[n][:], in_=w[n][:], func=ACT.Copy, scale=beta[:])
+                nc.sync.dma_start(out=out[:, NT * n : NT * (n + 1)], in_=w[n][:])
+        nc.vector.tensor_scalar(out=w[3][:], in0=w[3][:], scalar1=beta[:], scalar2=None, op0=ALU.mult)
+        nc.sync.dma_start(out=out[:, 3 * NT : D], in_=w[3][:])

@@ -47,7 +47,8 @@ def tile_robustaugmentation_w_kernel(
         kw_c = [keep.tile([P, 4 * NT], U8, name="kw_c%d" % j, align_bytes=64) for j in range(2)]
         vw = [keep.tile([P, 4 * D], U8, name="vw%d" % g, align_bytes=64) for g in range(VG - 2)]
         v_end = [keep.tile([P, 2, 4 * NT], U8, name="v_end%d" % n, align_bytes=64) for n in range(3)]
-        v_last = [keep.tile([P, 4 * NT], U8, name="v_last%d" % i, align_bytes=64) for i in range(2)]
+        v_six = keep.tile([P, 4 * NT], U8, name="v_six", align_bytes=64)
+        v_seven = [keep.tile([P, 2 * NT], U8, name="v_seven%d" % i, align_bytes=64) for i in range(2)]
 
         one = small("one")
         warm = small("warm")
@@ -98,8 +99,12 @@ def tile_robustaugmentation_w_kernel(
             nc.sync.dma_start(
                 out=v_end[n][:].bitcast(I32), in_=last_two[:, :, 4 * NT * n : 4 * NT * (n + 1)].bitcast(I32)
             )
-        for i in range(2):
-            nc.sync.dma_start(out=v_last[i][:].bitcast(I32), in_=value_words(VG - 2 + i, 3 * NT, D))
+        nc.sync.dma_start(out=v_six[:].bitcast(I32), in_=value_words(VG - 2, 3 * NT, D))
+        for n in (3, 4):
+            nc.sync.dma_start(
+                out=v_seven[n - 3][:].bitcast(I32),
+                in_=value_words(VG - 1, TILES[n][0], TILES[n][0] + TILES[n][1]),
+            )
 
         ss_s = small("ss_s")
         ss_v = small("ss_v")
@@ -293,10 +298,11 @@ def tile_robustaugmentation_w_kernel(
             if n == 2:
                 nc.vector.reduce_sum(out=rr_head[:], in_=rr[:, 0:3], axis=AX.X)
             dot_query(n)
-        for i in range(2):
-            for n in (3, 4):
-                c0, wd = TILES[n]
-                value_pass(n, VG - 2 + i, v_last[i][:, 4 * (c0 - 3 * NT) : 4 * (c0 - 3 * NT + wd)])
+        for n in (3, 4):
+            c0, wd = TILES[n]
+            value_pass(n, VG - 2, v_six[:, 4 * (c0 - 3 * NT) : 4 * (c0 - 3 * NT + wd)])
+        for n in (3, 4):
+            value_pass(n, VG - 1, v_seven[n - 3][:])
         sum_squares(3)
         nc.vector.tensor_scalar(out=rr_most[:], in0=rr[:, 3:4], scalar1=rr_head[:], scalar2=None, op0=ALU.add)
         sum_squares(4)
@@ -315,7 +321,9 @@ def tile_robustaugmentation_w_kernel(
             if n == 0:
                 nc.vector.reciprocal(out=beta[:], in_=root[:])
             if n < 3:
-                nc.scalar.activation(out=w[n][:], in_=w[n][:], func=ACT.Copy, scale=beta[:])
-                nc.sync.dma_start(out=out[:, NT * n : NT * (n + 1)], in_=w[n][:])
-        nc.vector.tensor_scalar(out=w[3][:], in0=w[3][:], scalar1=beta[:], scalar2=None, op0=ALU.mult)
-        nc.sync.dma_start(out=out[:, 3 * NT : D], in_=w[3][:])
+                nc.scalar.activation(out=w_cols(n), in_=w_cols(n), func=ACT.Copy, scale=beta[:])
+            else:
+                nc.vector.tensor_scalar(
+                    out=w_cols(n), in0=w_cols(n), scalar1=beta[:], scalar2=None, op0=ALU.mult
+                )
+            nc.sync.dma_start(out=out[:, TILES[n][0] : TILES[n][0] + TILES[n][1]], in_=w_cols(n))

from contextlib import ExitStack

import concourse.mybir as mybir
from concourse.masks import make_identity

F32 = mybir.dt.float32
BF16 = mybir.dt.bfloat16
U8 = mybir.dt.uint8
U32 = mybir.dt.uint32
I32 = mybir.dt.int32
FP8X4 = mybir.dt.float8_e4m3fn_x4
ALU = mybir.AluOpType
ACT = mybir.ActivationFunctionType
AX = mybir.AxisListType

P = 128
D = 2048
M = 4096
KG = D // 512
VG = M // 512
NT = 512
NA = 3072
TEMPERATURE = 0.07
TILES = ((0, 512), (512, 512), (1024, 512), (1536, 256), (1792, 256))

FLOPS = 2 * P * D * M * 2


def tile_robustaugmentation_w_kernel(
    tc, x, key_mem_words, key_mem_scales, value_mem_words, value_mem_scales, out
):
    nc = tc.nc
    with ExitStack() as ctx:
        keep = ctx.enter_context(tc.tile_pool(name="keep", bufs=1))
        psum = ctx.enter_context(tc.psum_pool(name="psum", bufs=1))
        ctx.enter_context(tc.manual_schedule())

        def small(name, cols=1):
            return keep.tile([P, cols], F32, name=name)

        x_sb = keep.tile([P, D], BF16, name="x_sb")
        ident = keep.tile([P, P], BF16, name="ident")
        k_planes = keep.tile([P, M], U8, name="k_planes", align_bytes=64)
        v_planes = keep.tile([P, 2 * D], U8, name="v_planes", align_bytes=64)
        kw_a = [keep.tile([P, 4 * NA], U8, name="kw_a%d" % g, align_bytes=64) for g in range(KG)]
        kw_b = keep.tile([P, KG - 1, 4 * (M - NA)], U8, name="kw_b", align_bytes=64)
        kw_c = [keep.tile([P, 4 * NT], U8, name="kw_c%d" % j, align_bytes=64) for j in range(2)]
        vw = [keep.tile([P, 4 * D], U8, name="vw%d" % g, align_bytes=64) for g in range(VG - 2)]
        v_end = [keep.tile([P, 2, 4 * NT], U8, name="v_end%d" % n, align_bytes=64) for n in range(3)]
        v_six = keep.tile([P, 4 * NT], U8, name="v_six", align_bytes=64)
        v_seven = [keep.tile([P, 2 * NT], U8, name="v_seven%d" % i, align_bytes=64) for i in range(2)]

        one = small("one")
        warm = small("warm")

        nc.vector.memset(k_planes[:].bitcast(I32), 0)
        nc.vector.memset(one[:], 1.0)
        nc.vector.memset(v_planes[:].bitcast(I32), 0)
        make_identity(nc, ident[:])
        nc.scalar.activation(out=warm[:], in_=one[:], func=ACT.Sqrt)

        def key_words(g, lo, hi):
            return key_mem_words[g].rearrange("p n t -> p (n t)")[:, 4 * lo : 4 * hi].bitcast(I32)

        def value_words(g, lo, hi):
            return value_mem_words[g].rearrange("p n t -> p (n t)")[:, 4 * lo : 4 * hi].bitcast(I32)

        def load_value_scales(h):
            for q in (0, 2, 1, 3):
                nc.sync.dma_start(
                    out=v_planes[32 * q : 32 * q + 16, D * h : D * (h + 1)].bitcast(I32),
                    in_=value_mem_scales[4 * h : 4 * h + 4, 4 * q : 4 * q + 4, :].bitcast(I32),
                )

        nc.sync.dma_start(out=x_sb[:], in_=x)
        for q in (0, 2, 1, 3):
            nc.sync.dma_start(
                out=k_planes[32 * q : 32 * q + 16, :].bitcast(I32),
                in_=key_mem_scales[:, 4 * q : 4 * q + 4, :].bitcast(I32),
            )
        for g in range(KG):
            nc.sync.dma_start(out=kw_a[g][:].bitcast(I32), in_=key_words(g, 0, NA))
        nc.sync.dma_start(
            out=kw_b[:].bitcast(I32),
            in_=key_mem_words[0 : KG - 1].rearrange("g p n t -> p g (n t)")[:, :, 4 * NA :].bitcast(I32),
        )
        for j in range(2):
            nc.sync.dma_start(
                out=kw_c[j][:].bitcast(I32), in_=key_words(3, NA + NT * j, NA + NT * (j + 1))
            )
        load_value_scales(0)
        for g in range(4):
            nc.sync.dma_start(out=vw[g][:].bitcast(I32), in_=value_words(g, 0, D))
        load_value_scales(1)
        for g in range(4, VG - 2):
            nc.sync.dma_start(out=vw[g][:].bitcast(I32), in_=value_words(g, 0, D))
        last_two = value_mem_words[VG - 2 : VG].rearrange("g p n t -> p g (n t)")
        for n in range(3):
            nc.sync.dma_start(
                out=v_end[n][:].bitcast(I32), in_=last_two[:, :, 4 * NT * n : 4 * NT * (n + 1)].bitcast(I32)
            )
        nc.sync.dma_start(out=v_six[:].bitcast(I32), in_=value_words(VG - 2, 3 * NT, D))
        for n in (3, 4):
            nc.sync.dma_start(
                out=v_seven[n - 3][:].bitcast(I32),
                in_=value_words(VG - 1, TILES[n][0], TILES[n][0] + TILES[n][1]),
            )

        ss_s = small("ss_s")
        ss_v = small("ss_v")
        norm = small("norm")
        rn = small("rn")
        junk_s = keep.tile([P, D // 2], BF16, name="junk_s")
        junk_v = keep.tile([P, D // 2], F32, name="junk_v")
        half = D // 2
        nc.scalar.activation(out=junk_s[:], in_=x_sb[:, 0:half], func=ACT.Square, accum_out=ss_s[:])
        nc.vector.scalar_tensor_tensor(
            out=junk_v[:], in0=x_sb[:, half:D], scalar=1.0, in1=x_sb[:, half:D],
            op0=ALU.mult, op1=ALU.mult, accum_out=ss_v[:],
        )
        nc.scalar.activation(out=norm[:], in_=ss_s[:], func=ACT.Sqrt, bias=ss_v[:])
        nc.vector.reciprocal(out=rn[:], in_=norm[:])

        q_bf = [keep.tile([P, 512], BF16, name="q_bf%d" % g) for g in range(KG)]
        q_t = [psum.tile([P, 4, P], BF16, name="q_t%d" % g, tag="bank%d" % g) for g in range(KG)]
        q_grp = [keep.tile([P, 1024], BF16, name="q_grp%d" % h, align_bytes=64) for h in range(2)]
        q_codes = [keep.tile([P, 256], U32, name="q_codes%d" % h, align_bytes=64) for h in range(2)]
        q_plane = [keep.tile([P, 256], U8, name="q_plane%d" % h, align_bytes=64) for h in range(2)]

        def sorted_view(ap):
            return ap.rearrange("b (t p) -> b t p", t=4)

        def natural_view(ap):
            return ap.rearrange("b (p t) -> b t p", t=4)

        def scale_query(g):
            src = natural_view(x_sb[:, 512 * g : 512 * (g + 1)])
            dst = sorted_view(q_bf[g][:])
            if g < 2:
                nc.vector.tensor_scalar(out=dst, in0=src, scalar1=rn[:], scalar2=None, op0=ALU.mult)
            else:
                nc.scalar.activation(out=dst, in_=src, func=ACT.Copy, scale=rn[:])

        def transpose_four(dst, src):
            for t in range(4):
                nc.tensor.transpose(out=dst[:, t, :], in_=src[:, P * t : P * (t + 1)], identity=ident[:])

        def group_query(g):
            dst = q_grp[g // 2][:, 512 * (g % 2) : 512 * (g % 2 + 1)].rearrange("p (b t) -> p b t", t=4)
            src = q_t[g][:].rearrange("p t b -> p b t")
            if g < 2:
                nc.vector.tensor_copy(out=dst, in_=src)
            else:
                nc.scalar.copy(out=dst, in_=src)

        for g in (0, 2, 1, 3):
            scale_query(g)
            transpose_four(q_t[g], q_bf[g])
        for g in (0, 2, 1, 3):
            group_query(g)
        for h in range(2):
            nc.vector.quantize_mx(out=q_codes[h][:].bitcast(FP8X4), scales=q_plane[h][:], in_=q_grp[h][:])

        q32 = keep.tile([P, D], F32, name="q32")
        nc.scalar.activation(out=q32[:], in_=x_sb[:], func=ACT.Copy, scale=rn[:])
        nc.scalar.activation(out=warm[:], in_=one[:], func=ACT.Exp)

        z = [psum.tile([P, NT], F32, name="z%d" % j, tag="bank%d" % j) for j in range(8)]
        zs = [keep.tile([P, NT], F32, name="zs%d" % j) for j in range(8)]
        nb = small("nb", 8)

        def key_pass(j, g, rhs):
            nc.tensor.matmul_mx(
                out=z[j][:],
                lhsT=q_codes[g // 2][:, P * (g % 2) : P * (g % 2 + 1)].bitcast(FP8X4),
                lhsT_scale=q_plane[g // 2][:, P * (g % 2) : P * (g % 2 + 1)],
                rhs=rhs.bitcast(FP8X4),
                rhs_scale=k_planes[4 * g : P, NT * j : NT * (j + 1)],
                start=(g == 0),
                stop=(g == KG - 1),
            )

        def leave_bank(j):
            nc.vector.tensor_scalar(
                out=sorted_view(zs[j][:]),
                in0=natural_view(z[j][:]),
                scalar1=-1.0 / TEMPERATURE,
                scalar2=(None if j == 0 else nb[:, j - 1 : j]),
                op0=ALU.mult,
                op1=ALU.min,
                accum_out=nb[:, j : j + 1],
            )

        na_banks = NA // NT
        for g in range(KG):
            for j in range(na_banks):
                key_pass(j, g, kw_a[g][:, 4 * NT * j : 4 * NT * (j + 1)])
        for j in range(na_banks):
            leave_bank(j)
        for g in range(KG - 1):
            for j in range(na_banks, 8):
                key_pass(j, g, kw_b[:, g, 4 * NT * (j - na_banks) : 4 * NT * (j - na_banks + 1)])
        for j in range(na_banks, 8):
            key_pass(j, KG - 1, kw_c[j - na_banks][:])
            leave_bank(j)

        e_sb = [keep.tile([P, 512], BF16, name="e_sb%d" % g) for g in range(VG)]
        e_grp = [keep.tile([P, 1024], BF16, name="e_grp%d" % u, align_bytes=64) for u in range(4)]
        e_codes = [keep.tile([P, 2 * P], U32, name="e_codes%d" % u, align_bytes=64) for u in range(4)]
        e_plane = [keep.tile([P, 2 * P], U8, name="e_plane%d" % u, align_bytes=64) for u in range(4)]
        e_t = {}
        r = [psum.tile([P, TILES[n][1]], F32, name="r%d" % n, tag="bank%d" % n) for n in range(5)]

        def exp_and_transpose(g):
            nc.scalar.activation(out=e_sb[g][:], in_=zs[g][:], func=ACT.Exp, scale=-1.0, bias=nb[:, 7:8])
            u = g // 2
            if g % 2 == 0:
                e_t[u] = psum.tile([P, 2, 4, P], BF16, name="e_t%d" % u, tag="bank%d" % (5 + u % 3))
            transpose_four(e_t[u][:, g % 2], e_sb[g])

        def group_e(u):
            nc.vector.tensor_copy(
                out=e_grp[u][:].rearrange("p (g b t) -> p g b t", g=2, t=4),
                in_=e_t[u][:].rearrange("p g t b -> p g b t"),
            )

        def quantise_e(u):
            nc.vector.quantize_mx(out=e_codes[u][:].bitcast(FP8X4), scales=e_plane[u][:], in_=e_grp[u][:])

        def value_pass(n, g, rhs):
            c0, wd = TILES[n]
            col = D * (g // 4) + c0
            nc.tensor.matmul_mx(
                out=r[n][:],
                lhsT=e_codes[g // 2][:, P * (g % 2) : P * (g % 2 + 1)].bitcast(FP8X4),
                lhsT_scale=e_plane[g // 2][:, P * (g % 2) : P * (g % 2 + 1)],
                rhs=rhs.bitcast(FP8X4),
                rhs_scale=v_planes[4 * (g % 4) : P, col : col + wd],
                start=(g == 0),
                stop=(g == VG - 1),
            )

        def whole_group(g):
            for n in range(5):
                c0, wd = TILES[n]
                value_pass(n, g, vw[g][:, 4 * c0 : 4 * (c0 + wd)])

        def four_chunks(first):
            for g in range(first, first + 4):
                exp_and_transpose(g)
            group_e(first // 2)
            quantise_e(first // 2)
            group_e(first // 2 + 1)
            quantise_e(first // 2 + 1)

        four_chunks(0)
        whole_group(0)
        whole_group(1)
        four_chunks(4)
        nc.scalar.activation(out=warm[:], in_=one[:], func=ACT.Sqrt)
        for g in range(2, VG - 2):
            whole_group(g)

        rr = small("rr", 5)
        qr = small("qr", 5)
        rr_head = small("rr_head")
        rr_most = small("rr_most")
        rho = small("rho")
        qr_sum = small("qr_sum")
        v2 = small("v2")
        root = small("root")
        beta = small("beta")
        w = [keep.tile([P, NT], F32, name="w%d" % n) for n in range(4)]

        def q_cols(n):
            c0, wd = TILES[n]
            return q32[:, c0 : c0 + wd]

        def w_cols(n):
            c0, wd = TILES[n]
            return w[c0 // NT][:, c0 % NT : c0 % NT + wd]

        def sum_squares(n):
            wd = TILES[n][1]
            nc.scalar.activation(out=junk_s[:, 0:wd], in_=r[n][:], func=ACT.Square, accum_out=rr[:, n : n + 1])

        def dot_query(n):
            wd = TILES[n][1]
            nc.vector.scalar_tensor_tensor(
                out=junk_v[:, 0:wd], in0=r[n][:], scalar=1.0, in1=q_cols(n),
                op0=ALU.mult, op1=ALU.mult, accum_out=qr[:, n : n + 1],
            )

        for n in range(3):
            for i in range(2):
                value_pass(n, VG - 2 + i, v_end[n][:, i, :])
            sum_squares(n)
            if n == 2:
                nc.vector.reduce_sum(out=rr_head[:], in_=rr[:, 0:3], axis=AX.X)
            dot_query(n)
        for n in (3, 4):
            c0, wd = TILES[n]
            value_pass(n, VG - 2, v_six[:, 4 * (c0 - 3 * NT) : 4 * (c0 - 3 * NT + wd)])
        for n in (3, 4):
            value_pass(n, VG - 1, v_seven[n - 3][:])
        sum_squares(3)
        nc.vector.tensor_scalar(out=rr_most[:], in0=rr[:, 3:4], scalar1=rr_head[:], scalar2=None, op0=ALU.add)
        sum_squares(4)
        nc.scalar.activation(out=rho[:], in_=rr[:, 4:5], func=ACT.Sqrt, bias=rr_most[:])
        dot_query(3)
        dot_query(4)
        nc.vector.reduce_sum(out=qr_sum[:], in_=qr[:], axis=AX.X)
        nc.vector.tensor_scalar(
            out=v2[:], in0=qr_sum[:], scalar1=rho[:], scalar2=rho[:], op0=ALU.add, op1=ALU.mult
        )
        nc.scalar.activation(out=root[:], in_=v2[:], func=ACT.Sqrt, scale=2.0)
        for n in range(5):
            nc.vector.scalar_tensor_tensor(
                out=w_cols(n), in0=q_cols(n), scalar=rho[:], in1=r[n][:], op0=ALU.mult, op1=ALU.add
            )
            if n == 0:
                nc.vector.reciprocal(out=beta[:], in_=root[:])
            if n < 3:
                nc.scalar.activation(out=w_cols(n), in_=w_cols(n), func=ACT.Copy, scale=beta[:])
            else:
                nc.vector.tensor_scalar(
                    out=w_cols(n), in0=w_cols(n), scalar1=beta[:], scalar2=None, op0=ALU.mult
                )
            nc.sync.dma_start(out=out[:, TILES[n][0] : TILES[n][0] + TILES[n][1]], in_=w_cols(n))
